import numpy as np
import ml_dtypes


def mxq(x, axis, fmt="e4m3"):
    dtype, down = {"e4m3": (ml_dtypes.float8_e4m3fn, 7), "e5m2": (ml_dtypes.float8_e5m2, 14)}[fmt]
    v = np.moveaxis(np.asarray(x, np.float32).astype(ml_dtypes.bfloat16).astype(np.float64), axis, -1)
    blocks = v.reshape(v.shape[:-1] + (-1, 32))
    amax = np.abs(blocks).max(-1, keepdims=True)
    byte = np.maximum(np.where(amax > 0, np.frexp(amax)[1] - 1 + 127, 0) - down, 1)
    scale = np.exp2(byte - 127.0)
    codes = (blocks / scale).astype(np.float32).astype(dtype).astype(np.float64)
    return np.moveaxis((codes * scale).reshape(v.shape), -1, axis)


WIDE = False


def mx_kscale(k):
    if not WIDE:
        return np.ones(k)
    levels = np.array([10, -10, 5, -5, 0])
    if k % 512:
        return np.exp2(np.random.permutation(np.resize(levels, k // 32))).repeat(32)
    a = np.empty((k // 512, 16))
    for p in range(k // 512):
        a[p, :8] = np.random.permutation(np.resize(levels, 8))
        for g in range(8):
            far = levels[np.abs(levels - a[p, g]) >= 10]
            a[p, g + 8] = far[np.random.randint(len(far))]
    return np.exp2(a.ravel()).repeat(32)


BF16 = ml_dtypes.bfloat16


def bf(x):
    return np.asarray(x, np.float32).astype(BF16)


def f64(x):
    return np.asarray(x).astype(np.float64)


B, S, D, H, DH, F = 4, 1024, 1024, 4, 128, 512
E = H * DH
EPS = 1e-5
NTERMS = 120


def layernorm(x, g, b):
    mu = x.mean(-1, keepdims=True)
    var = np.square(x - mu).mean(-1, keepdims=True)
    return (x - mu) / np.sqrt(var + EPS) * g + b


def erf(v):
    a = np.minimum(np.maximum(v, -6.0), 6.0)
    term = a.copy()
    total = a.copy()
    for n in range(1, NTERMS):
        term = term * (2.0 * a * a) / (2.0 * n + 1.0)
        total = total + term
    return 2.0 / np.sqrt(np.pi) * np.exp(-a * a) * total


def gelu_erf(v):
    return 0.5 * v * (1.0 + erf(v / np.sqrt(2.0)))


def draw0():
    s, t = mx_kscale(E), mx_kscale(D)
    x = np.random.standard_normal((B, S, D)) + 0.5 * np.random.standard_normal((B, S, 1))
    return {"h_attn": bf(0.2 * np.random.standard_normal((B, S, E)) * s),
            "x": bf(x),
            "w_out": bf(np.random.standard_normal((D, E)) * 2.0 / np.sqrt(E) / s),
            "w_fc1": bf(np.random.standard_normal((F, D)) / np.sqrt(D) / t),
            "g2": bf((1.0 + 0.1 * np.random.standard_normal(D)) * t),
            "b2": bf(0.1 * np.random.standard_normal(D) * t)}


def core(h_attn, x, w_out, w_fc1, g2, b2):
    x_mid = f64(x) + (mxq(f64(h_attn), 2, "e4m3") @ mxq(f64(w_out), 1, "e4m3").T)
    h = layernorm(x_mid, f64(g2), f64(b2))
    u = mxq(h, 2, "e4m3") @ mxq(f64(w_fc1), 1, "e4m3").T
    return x_mid, gelu_erf(u)


def e4m3fn_bytes(y):
    return np.clip(np.asarray(y, np.float64), -448.0, 448.0).astype(np.float32).astype(ml_dtypes.float8_e4m3fn).view(np.uint8)


def e4m3fn_values(b):
    return np.asarray(b, np.uint8).view(ml_dtypes.float8_e4m3fn).astype(np.float64)


def setup_inputs():
    d = draw0()
    x0 = np.asarray(d['h_attn']).astype(np.float64)
    s = (np.max(np.abs(x0), axis=(0, 1), keepdims=True) / 448.0).astype(np.float32)
    out = {}
    for k, v in d.items():
        if k == 'h_attn':
            out['h_attn_bytes'] = e4m3fn_bytes(x0 / s.astype(np.float64))
            out['h_attn_scale'] = s
        else:
            out[k] = v
    return out


def reference(h_attn_bytes, h_attn_scale, x, w_out, w_fc1, g2, b2):
    return core(e4m3fn_values(h_attn_bytes) * h_attn_scale.astype(np.float64), x, w_out, w_fc1, g2, b2)

@@ -1,0 +1,376 @@
+from contextlib import ExitStack
+
+import concourse.mybir as mybir
+from concourse.masks import make_identity
+
+TOKENS, D, E, F = 4096, 1024, 512, 512
+EPS = 1e-5
+FLOPS = 2 * TOKENS * E * D + 2 * TOKENS * D * F
+
+F32 = mybir.dt.float32
+BF16 = mybir.dt.bfloat16
+U32 = mybir.dt.uint32
+U8 = mybir.dt.uint8
+FP8 = mybir.dt.float8_e4m3fn
+FP8X4 = mybir.dt.float8_e4m3fn_x4
+ALU = mybir.AluOpType
+ACT = mybir.ActivationFunctionType
+
+P = 128
+N_TILES = TOKENS // P
+GROUPS = [4,4,4,4,4,4,4,2,2]
+Z_ENGINE = "vector"
+LP, LT, ZLAG = 6, 5, 2
+
+
+def tile_minitransformerlayer_pb_t_kernel(tc, h_attn_bytes, h_attn_scale, x, w_out, w_fc1, g2, b2, out_0, out_1):
+    nc = tc.nc
+    hb_rows = h_attn_bytes.flatten_outer_dims()
+    x_rows = x.flatten_outer_dims()
+    mid_rows = out_0.flatten_outer_dims()
+    act_rows = out_1.flatten_outer_dims()
+
+    bases = []
+    base = 0
+    for n in GROUPS:
+        bases.append(base)
+        base += n
+
+    group_of = {}
+    for gi, n in enumerate(GROUPS):
+        for j in range(n):
+            group_of[bases[gi] + j] = (gi, j)
+
+    with ExitStack() as ctx:
+        keep = ctx.enter_context(tc.tile_pool(name="keep", bufs=1))
+        stage = ctx.enter_context(tc.tile_pool(name="stage", bufs=1))
+        work = ctx.enter_context(tc.tile_pool(name="work", bufs=2))
+        psum = ctx.enter_context(tc.psum_pool(name="psum", bufs=2))
+        ctx.enter_context(tc.manual_schedule())
+
+        ident = keep.tile([P, P], F32, name="ident")
+        make_identity(nc, ident[:])
+        scale_rows = keep.tile([P, E], F32, name="scale_rows")
+        gb_bf = keep.tile([P, P], BF16, name="gb_bf")
+        gb_f = keep.tile([P, P], F32, name="gb_f")
+        gb = keep.tile([P, 16], F32, name="gb")
+        mhalf = keep.tile([P, 1], F32, name="mhalf")
+        nc.gpsimd.memset(gb_bf[:], 0.0)
+        nc.gpsimd.memset(mhalf[:], -0.5)
+
+        wo_codes = keep.tile([P, D], U32, name="wo_codes", align_bytes=64)
+        wo_scales = keep.tile([P, D], U8, name="wo_scales", align_bytes=64)
+        wf_codes = keep.tile([P, 2, F], U32, name="wf_codes", align_bytes=64)
+        wf_scales = keep.tile([P, 2, F], U8, name="wf_scales", align_bytes=64)
+
+        bytes_t = {}
+        x_t = {}
+
+        def rows_of(dram, gi):
+            b, n = bases[gi], GROUPS[gi]
+            return dram[P * b : P * (b + n), :].rearrange("(p j) k -> p j k", j=n)
+
+        def load_bytes(gi):
+            bytes_t[gi] = keep.tile([P, GROUPS[gi], E], U8, name="bytes_%d" % gi)
+            nc.sync.dma_start(out=bytes_t[gi][:], in_=rows_of(hb_rows, gi))
+
+        def load_x(gi, split=1):
+            n = GROUPS[gi]
+            xt = work.tile([P, n, D], BF16, name="xt", bufs=3)
+            x_t[gi] = xt
+            for c in range(split):
+                js = slice(c * n // split, (c + 1) * n // split)
+                nc.sync.dma_start(out=xt[:, js, :], in_=rows_of(x_rows, gi)[:, js, :])
+
+        load_bytes(0)
+        nc.scalar.dma_start(out=scale_rows[:], in_=h_attn_scale.rearrange("a b k -> (a b k)").partition_broadcast(P))
+        wo_raw = stage.tile([P, 8, E], BF16, name="wo_raw", tag="w8", bufs=3, align_bytes=64)
+        wo_view = w_out.rearrange("(a p) k -> p a k", p=P)
+        for c in range(2):
+            nc.sync.dma_start(out=wo_raw[:, 4 * c : 4 * c + 4, :], in_=wo_view[:, 4 * c : 4 * c + 4, :])
+        load_x(0, 4)
+        for v, vec in enumerate((g2, b2)):
+            view = vec.rearrange("(g q t r) -> g t q r", g=2, q=16, t=4)
+            for g in range(2):
+                r0 = 8 * v + 4 * g
+                nc.scalar.dma_start(out=gb_bf[r0 : r0 + 4, :].rearrange("t (q r) -> t q r", q=16), in_=view[g])
+        load_bytes(1)
+        wf_raw = stage.tile([P, 4, D], BF16, name="wf_raw", tag="w8", bufs=3, align_bytes=64)
+        nc.sync.dma_start(out=wf_raw[:], in_=w_fc1.rearrange("(a p) k -> p a k", p=P))
+        load_x(1)
+        load_bytes(2)
+
+        def turn(bank, slot, words, start):
+            for u in range(2):
+                c0 = P * (2 * slot + u)
+                nc.tensor.transpose(bank[:, c0 : c0 + P], words[:, start + u : start + 256 : 2], ident[:])
+
+        def empty_words(bank, dst, engine):
+            out = dst.rearrange("p n j -> p (n j)").bitcast(F32).rearrange("p (b r u) -> p b r u", b=2, u=2)
+            in_ = bank[:].rearrange("p (b u r) -> p b r u", b=2, u=2)
+            if engine == "v":
+                nc.vector.tensor_copy(out=out, in_=in_)
+            else:
+                nc.scalar.copy(out=out, in_=in_)
+
+        def quantize(codes, scales, src):
+            nc.vector.quantize_mx(out=codes.bitcast(FP8X4), scales=scales, in_=src.rearrange("p n j -> p (n j)"))
+
+        hb_t = {}
+        a_bank = {}
+        a_grp = {}
+        a_codes = {}
+        a_scales = {}
+
+        def a_product(i):
+            gi, j = group_of[i]
+            hb = work.tile([P, E], BF16, name="hb", bufs=6)
+            hb_t[i] = hb
+            nc.vector.tensor_tensor(out=hb[:], in0=bytes_t[gi][:, j, :].bitcast(FP8), in1=scale_rows[:], op=ALU.mult)
+
+        def a_turn(i):
+            if i % 2 == 0:
+                bank = psum.tile([P, 512], F32, name="pa", bufs=1)
+                a_bank[i // 2] = bank
+            turn(a_bank[i // 2], i % 2, hb_t.pop(i)[:].bitcast(F32), 0)
+
+        def a_empty(pair, engine="s"):
+            grp = work.tile([P, 256, 4], BF16, name="a_grp", bufs=3, align_bytes=64)
+            a_grp[pair] = grp
+            empty_words(a_bank.pop(pair), grp[:], engine)
+
+        def a_quant(pair):
+            codes = work.tile([P, 256], U32, name="a_codes", bufs=3, align_bytes=64)
+            scales = work.tile([P, 256], U8, name="a_scales", bufs=3, align_bytes=64)
+            a_codes[pair], a_scales[pair] = codes, scales
+            quantize(codes[:], scales[:], a_grp.pop(pair)[:])
+
+        m1 = {}
+        xm_t = {}
+        nm_t = {}
+        rs_t = {}
+        z_t = {}
+
+        def mm1(i):
+            pair, h = divmod(i, 2)
+            cs = slice(P * h, P * h + P)
+            m1[i] = []
+            for c in range(2):
+                bank = psum.tile([P, 512], F32, name="pm", bufs=3)
+                m1[i].append(bank)
+                ds = slice(512 * c, 512 * c + 512)
+                nc.tensor.matmul_mx(
+                    out=bank[:],
+                    lhsT=a_codes[pair][:, cs].bitcast(FP8X4),
+                    lhsT_scale=a_scales[pair][:, cs],
+                    rhs=wo_codes[:, ds].bitcast(FP8X4),
+                    rhs_scale=wo_scales[:, ds],
+                    start=True,
+                    stop=True,
+                )
+
+        sums = {}
+
+        def residual(i):
+            gi, j = group_of[i]
+            xm = work.tile([P, D], F32, name="xm", bufs=7)
+            sm = work.tile([P, 2], F32, name="sm", bufs=4)
+            xm_t[i], sums[i] = xm, sm
+            for c in range(2):
+                ds = slice(512 * c, 512 * c + 512)
+                nc.vector.scalar_tensor_tensor(
+                    out=xm[:, ds], in0=m1[i][c][:], scalar=1.0, in1=x_t[gi][:, j, ds],
+                    op0=ALU.mult, op1=ALU.add, accum_out=sm[:, c : c + 1],
+                )
+            nc.sync.dma_start(out=rows_of(mid_rows, gi)[:, j, :], in_=xm[:])
+
+        def neg_mean(i):
+            nm = work.tile([P, 1], F32, name="nm", bufs=6)
+            nm_t[i] = nm
+            sm = sums.pop(i)
+            nc.vector.tensor_scalar(out=nm[:], in0=sm[:, 0:1], scalar1=sm[:, 1:2], scalar2=-1.0 / D, op0=ALU.add, op1=ALU.mult)
+
+        def deviation(i):
+            junk = work.tile([P, D], BF16, name="junk", bufs=2)
+            ss = work.tile([P, 1], F32, name="ss", bufs=4)
+            nc.scalar.activation(out=junk[:], in_=xm_t[i][:], func=ACT.Square, bias=nm_t[i][:], scale=1.0, accum_out=ss[:])
+            ve = work.tile([P, 1], F32, name="ve", bufs=4)
+            rs = work.tile([P, 1], F32, name="rs", bufs=6)
+            rs_t[i] = rs
+            nc.gpsimd.tensor_scalar(out=ve[:], in0=ss[:], scalar1=1.0 / D, scalar2=EPS, op0=ALU.mult, op1=ALU.add)
+            nc.gpsimd.tensor_tensor(out=rs[:], in0=ve[:], in1=mhalf[:], op=ALU.pow)
+
+        def normalize(i):
+            z = work.tile([P, D], F32, name="z", bufs=9)
+            z_t[i] = z
+            eng = nc.vector if Z_ENGINE == "vector" else nc.gpsimd
+            eng.tensor_scalar(
+                out=z[:].rearrange("p (t q r) -> p t q r", t=4, r=8),
+                in0=xm_t.pop(i)[:].rearrange("p (q t r) -> p t q r", t=4, r=8),
+                scalar1=nm_t.pop(i)[:], scalar2=rs_t.pop(i)[:], op0=ALU.add, op1=ALU.mult,
+            )
+
+        planes = {}
+        inter = {}
+        h_codes = {}
+        h_scales = {}
+
+        def plane(gi, idx, engine):
+            g, t = divmod(idx, 4)
+            n = GROUPS[gi]
+            if t == 0:
+                hp = work.tile([P, 4, P * n], BF16, name="hp", bufs=4)
+                planes[gi, g] = hp
+            bank = psum.tile([P, P * n], F32, name="pz", bufs=2)
+            for j in range(n):
+                c0 = 256 * t + P * g
+                nc.tensor.transpose(bank[:, P * j : P * j + P], z_t[bases[gi] + j][:, c0 : c0 + P], ident[:])
+            dst = planes[gi, g][:, t, :]
+            if engine == "v":
+                nc.vector.tensor_scalar(out=dst, in0=bank[:], scalar1=gb[:, idx : idx + 1], scalar2=gb[:, 8 + idx : 9 + idx], op0=ALU.mult, op1=ALU.add)
+            else:
+                nc.scalar.activation(out=dst, in_=bank[:], func=ACT.Identity, bias=gb[:, 8 + idx : 9 + idx], scale=gb[:, idx : idx + 1])
+
+        def interleave(gi, g):
+            n = GROUPS[gi]
+            hi = work.tile([P, P * n, 4], BF16, name="hi", bufs=3, align_bytes=64)
+            inter[gi, g] = hi
+            nc.vector.tensor_copy(
+                out=hi[:].rearrange("p (c i) t -> p c t i", i=4),
+                in_=planes.pop((gi, g))[:].rearrange("p t (c i) -> p c t i", i=4),
+            )
+
+        def h_quant(gi, g):
+            n = GROUPS[gi]
+            codes = work.tile([P, P * n], U32, name="h_codes", bufs=6, align_bytes=64)
+            scales = work.tile([P, P * n], U8, name="h_scales", bufs=6, align_bytes=64)
+            h_codes[gi, g], h_scales[gi, g] = codes, scales
+            quantize(codes[:], scales[:], inter.pop((gi, g))[:])
+
+        def mm2(i):
+            gi, j = group_of[i]
+            bank = psum.tile([P, F], F32, name="pu", bufs=2)
+            cs = slice(P * j, P * j + P)
+            for g in range(2):
+                nc.tensor.matmul_mx(
+                    out=bank[:],
+                    lhsT=h_codes[gi, g][:, cs].bitcast(FP8X4),
+                    lhsT_scale=h_scales[gi, g][:, cs],
+                    rhs=wf_codes[:, g, :].bitcast(FP8X4),
+                    rhs_scale=wf_scales[:, g, :],
+                    start=(g == 0),
+                    stop=(g == 1),
+                )
+            return bank
+
+        def gelu(i, bank):
+            gi, j = group_of[i]
+            act = work.tile([P, F], F32, name="act", bufs=4)
+            nc.scalar.activation(out=act[:], in_=bank[:], func=ACT.Gelu)
+            nc.sync.dma_start(out=rows_of(act_rows, gi)[:, j, :], in_=act[:])
+
+        wo_grp = stage.tile([P, D, 4], BF16, name="wo_grp", tag="w8", bufs=3, align_bytes=64)
+        wo_words = wo_raw[:].rearrange("p a k -> p (a k)").bitcast(F32)
+        for i in range(LP):
+            a_product(i)
+        for i in range(2):
+            a_turn(i)
+        a_empty(0)
+        for c in range(4):
+            if c % 2 == 0:
+                bank = psum.tile([P, 512], F32, name="pz", bufs=2)
+            else:
+                bank = psum.tile([P, 512], F32, name="pu", bufs=2)
+            for b in range(2):
+                turn(bank, b, wo_words, 256 * (2 * c + b))
+            empty_words(bank, wo_grp[:, 256 * c : 256 * c + 256, :], "vs"[c % 2])
+            if c == 1:
+                a_quant(0)
+                for i in range(2, 4):
+                    a_turn(i)
+                a_empty(1)
+                quantize(wo_codes[:, 0:512], wo_scales[:, 0:512], wo_grp[:, 0:512, :])
+        for i in range(4, LT):
+            a_turn(i)
+        quantize(wo_codes[:, 512:1024], wo_scales[:, 512:1024], wo_grp[:, 512:1024, :])
+        a_quant(1)
+        mm1(0)
+        nc.scalar.copy(out=gb_f[:], in_=gb_bf[:])
+        bank = psum.tile([P, 512], F32, name="pz", bufs=2)
+        nc.tensor.transpose(bank[:, 0:P], gb_f[:], ident[:])
+        nc.scalar.copy(out=gb[:], in_=bank[:, 0:16])
+
+        wf_perm = stage.tile([P, 4, D], BF16, name="wf_perm", tag="w8", bufs=3, align_bytes=64)
+        wf_grp = stage.tile([P, 2, F, 4], BF16, name="wf_grp", tag="w8", bufs=3, align_bytes=64)
+        wf_words = wf_perm[:].rearrange("p a k -> p (a k)").bitcast(F32)
+
+        def wf_permute(a):
+            nc.scalar.copy(
+                out=wf_perm[:, a, :].rearrange("p (q r t) -> p q r t", r=8, t=4),
+                in_=wf_raw[:, a, :].rearrange("p (q t r) -> p q r t", r=8, t=4),
+            )
+
+        def wf_turn(g, half):
+            bank = psum.tile([P, 512], F32, name="pu", bufs=2)
+            for b in range(2):
+                turn(bank, b, wf_words, 512 * (2 * half + b) + 256 * g)
+            empty_words(bank, wf_grp[:, g, 256 * half : 256 * half + 256, :], "s")
+
+        plane_at = {}
+        inter_at = {}
+        quant_at = {}
+        mm2_at = {}
+        last_slot = 0
+        for gi, n in enumerate(GROUPS):
+            e = bases[gi] + n - 1 + ZLAG - 1
+            per = 8 // n
+            for s in range(n):
+                plane_at.setdefault(e + 2 + s, []).extend((gi, per * s + k) for k in range(per))
+            inter_at.setdefault(e + 2 + n // 2, []).append((gi, 0))
+            inter_at.setdefault(e + 2 + n, []).append((gi, 1))
+            quant_at.setdefault(e + 3 + n // 2, []).append((gi, 0))
+            quant_at.setdefault(e + 3 + n, []).append((gi, 1))
+            for j in range(n):
+                mm2_at.setdefault(e + 4 + n + j, []).append(bases[gi] + j)
+                last_slot = max(last_slot, e + 4 + n + j)
+
+        for s in range(last_slot + 1):
+            for gi in range(2, len(GROUPS)):
+                if s == max(0, bases[gi] - 7):
+                    load_x(gi)
+                    if gi + 1 < len(GROUPS):
+                        load_bytes(gi + 1)
+            if s + 1 < N_TILES:
+                mm1(s + 1)
+            u_banks = [(i, mm2(i)) for i in mm2_at.get(s, [])]
+            if s % 2 == 1 and (s + 4) < N_TILES:
+                a_quant((s + 4) // 2)
+            if s < N_TILES:
+                residual(s)
+            if 0 <= s - ZLAG < N_TILES:
+                normalize(s - ZLAG)
+            if s < N_TILES:
+                neg_mean(s)
+            for gi, g in quant_at.get(s, []):
+                h_quant(gi, g)
+            if s + LP < N_TILES:
+                a_product(s + LP)
+            if 2 <= s < 6:
+                wf_turn(s % 2, s // 2 - 1)
+            if s + LT < N_TILES:
+                a_turn(s + LT)
+            for k, (gi, idx) in enumerate(plane_at.get(s, [])):
+                plane(gi, idx, "v" if (s >= N_TILES and k % 2 == 1) else "s")
+            for i, bank in u_banks:
+                gelu(i, bank)
+            if s % 2 == 0 and s + LT < N_TILES:
+                a_empty((s + LT) // 2)
+            if s < N_TILES:
+                deviation(s)
+            if s < 4:
+                wf_permute(s)
+            for gi, g in inter_at.get(s, []):
+                interleave(gi, g)
+            if s in (6, 7):
+                g = s - 6
+                quantize(wf_codes[:, g, :], wf_scales[:, g, :], wf_grp[:, g, :, :])

@@ -19,8 +19,11 @@ ACT = mybir.ActivationFunctionType
 P = 128
 N_TILES = TOKENS // P
 GROUPS = [4,4,4,4,4,4,4,2,2]
-Z_ENGINE = "vector"
-LP, LT, ZLAG = 6, 5, 2
+Z_ENGINE = "gpsimd"
+LP, ZLAG, WF = 7, 2, 3
+AQ = 2
+IL, QL, ML = 1, 1, 1
+VG, VIDX = 7, (1, 3, 5, 7)
 
 
 def tile_minitransformerlayer_pb_t_kernel(tc, h_attn_bytes, h_attn_scale, x, w_out, w_fc1, g2, b2, out_0, out_1):
@@ -271,29 +274,21 @@ def tile_minitransformerlayer_pb_t_kernel(tc, h_attn_bytes, h_attn_scale, x, w_o
 
         wo_grp = stage.tile([P, D, 4], BF16, name="wo_grp", tag="w8", bufs=3, align_bytes=64)
         wo_words = wo_raw[:].rearrange("p a k -> p (a k)").bitcast(F32)
-        for i in range(LP):
+        for i in range(2):
             a_product(i)
         for i in range(2):
             a_turn(i)
-        a_empty(0)
         for c in range(4):
-            if c % 2 == 0:
-                bank = psum.tile([P, 512], F32, name="pz", bufs=2)
-            else:
-                bank = psum.tile([P, 512], F32, name="pu", bufs=2)
+            bank = psum.tile([P, 512], F32, name=("pz", "pu")[c % 2], bufs=2)
             for b in range(2):
                 turn(bank, b, wo_words, 256 * (2 * c + b))
             empty_words(bank, wo_grp[:, 256 * c : 256 * c + 256, :], "vs"[c % 2])
+            if c == 0:
+                a_empty(0)
             if c == 1:
-                a_quant(0)
-                for i in range(2, 4):
-                    a_turn(i)
-                a_empty(1)
                 quantize(wo_codes[:, 0:512], wo_scales[:, 0:512], wo_grp[:, 0:512, :])
-        for i in range(4, LT):
-            a_turn(i)
+                a_quant(0)
         quantize(wo_codes[:, 512:1024], wo_scales[:, 512:1024], wo_grp[:, 512:1024, :])
-        a_quant(1)
         mm1(0)
         nc.scalar.copy(out=gb_f[:], in_=gb_bf[:])
         bank = psum.tile([P, 512], F32, name="pz", bufs=2)
@@ -326,13 +321,27 @@ def tile_minitransformerlayer_pb_t_kernel(tc, h_attn_bytes, h_attn_scale, x, w_o
             per = 8 // n
             for s in range(n):
                 plane_at.setdefault(e + 2 + s, []).extend((gi, per * s + k) for k in range(per))
-            inter_at.setdefault(e + 2 + n // 2, []).append((gi, 0))
-            inter_at.setdefault(e + 2 + n, []).append((gi, 1))
-            quant_at.setdefault(e + 3 + n // 2, []).append((gi, 0))
-            quant_at.setdefault(e + 3 + n, []).append((gi, 1))
+            half = (n - 1) // 2
+            for g, done in enumerate((e + 2 + half, e + 1 + n)):
+                inter_at.setdefault(done + IL, []).append((gi, g))
+                quant_at.setdefault(done + IL + QL, []).append((gi, g))
             for j in range(n):
-                mm2_at.setdefault(e + 4 + n + j, []).append(bases[gi] + j)
-                last_slot = max(last_slot, e + 4 + n + j)
+                at = e + 1 + n + IL + QL + ML + j
+                mm2_at.setdefault(at, []).append(bases[gi] + j)
+                last_slot = max(last_slot, at)
+
+        product_at = {}
+        turn_at = {}
+        empty_at = {}
+        a_quant_at = {}
+        for i in range(2, N_TILES):
+            ps = max(i - LP, i // 2 - 1)
+            ts = 0 if i < 4 else max(i - LP + 1, i // 2)
+            product_at.setdefault(ps, []).append(i)
+            turn_at.setdefault(ts, []).append(i)
+            if i % 2 == 1:
+                empty_at[ts] = i // 2
+                a_quant_at[min(ts + AQ, i - 2)] = i // 2
 
         for s in range(last_slot + 1):
             for gi in range(2, len(GROUPS)):
@@ -340,37 +349,41 @@ def tile_minitransformerlayer_pb_t_kernel(tc, h_attn_bytes, h_attn_scale, x, w_o
                     load_x(gi)
                     if gi + 1 < len(GROUPS):
                         load_bytes(gi + 1)
+            if s in a_quant_at:
+                a_quant(a_quant_at[s])
             if s + 1 < N_TILES:
                 mm1(s + 1)
             u_banks = [(i, mm2(i)) for i in mm2_at.get(s, [])]
-            if s % 2 == 1 and (s + 4) < N_TILES:
-                a_quant((s + 4) // 2)
             if s < N_TILES:
                 residual(s)
             if 0 <= s - ZLAG < N_TILES:
                 normalize(s - ZLAG)
+            for n_p, i in enumerate(product_at.get(s, [])):
+                if n_p == 0:
+                    a_product(i)
             if s < N_TILES:
                 neg_mean(s)
             for gi, g in quant_at.get(s, []):
                 h_quant(gi, g)
-            if s + LP < N_TILES:
-                a_product(s + LP)
-            if 2 <= s < 6:
-                wf_turn(s % 2, s // 2 - 1)
-            if s + LT < N_TILES:
-                a_turn(s + LT)
+            for n_p, i in enumerate(product_at.get(s, [])):
+                if n_p > 0:
+                    a_product(i)
+            if WF <= s < WF + 4:
+                wf_turn((s - WF) % 2, (s - WF) // 2)
+            for i in turn_at.get(s, []):
+                a_turn(i)
             for k, (gi, idx) in enumerate(plane_at.get(s, [])):
-                plane(gi, idx, "v" if (s >= N_TILES and k % 2 == 1) else "s")
+                plane(gi, idx, "v" if (gi >= VG and idx % 8 in VIDX) else "s")
             for i, bank in u_banks:
                 gelu(i, bank)
-            if s % 2 == 0 and s + LT < N_TILES:
-                a_empty((s + LT) // 2)
+            if s in empty_at:
+                a_empty(empty_at[s])
             if s < N_TILES:
                 deviation(s)
-            if s < 4:
-                wf_permute(s)
+            if WF - 2 <= s < WF + 2:
+                wf_permute(s - WF + 2)
             for gi, g in inter_at.get(s, []):
                 interleave(gi, g)
-            if s in (6, 7):
-                g = s - 6
+            if s in (WF + 4, WF + 5):
+                g = s - WF - 4
                 quantize(wf_codes[:, g, :], wf_scales[:, g, :], wf_grp[:, g, :, :])

@@ -20,10 +20,12 @@ P = 128
 N_TILES = TOKENS // P
 GROUPS = [4,4,4,4,4,4,4,2,2]
 Z_ENGINE = "gpsimd"
-LP, ZLAG, WF = 7, 2, 3
+LP, WF = 8, 3
 AQ = 2
-IL, QL, ML = 1, 1, 1
-VG, VIDX = 7, (1, 3, 5, 7)
+ZB = 12
+TL, DL, IL, QL, ML, GL = 4, 1, 1, 1, 1, 1
+RB = 2
+VG, VIDX, VTAIL = 6, (), (2, 5, 7)
 
 
 def tile_minitransformerlayer_pb_t_kernel(tc, h_attn_bytes, h_attn_scale, x, w_out, w_fc1, g2, b2, out_0, out_1):
@@ -57,7 +59,7 @@ def tile_minitransformerlayer_pb_t_kernel(tc, h_attn_bytes, h_attn_scale, x, w_o
         gb_bf = keep.tile([P, P], BF16, name="gb_bf")
         gb_f = keep.tile([P, P], F32, name="gb_f")
         gb = keep.tile([P, 16], F32, name="gb")
-        mhalf = keep.tile([P, 1], F32, name="mhalf")
+        mhalf = keep.tile([P, RB], F32, name="mhalf")
         nc.gpsimd.memset(gb_bf[:], 0.0)
         nc.gpsimd.memset(mhalf[:], -0.5)
 
@@ -69,21 +71,19 @@ def tile_minitransformerlayer_pb_t_kernel(tc, h_attn_bytes, h_attn_scale, x, w_o
         bytes_t = {}
         x_t = {}
 
-        def rows_of(dram, gi):
-            b, n = bases[gi], GROUPS[gi]
-            return dram[P * b : P * (b + n), :].rearrange("(p j) k -> p j k", j=n)
+        def rows_of(dram, li):
+            return dram[4 * P * li : 4 * P * (li + 1), :].rearrange("(p j) k -> p j k", j=4)
 
-        def load_bytes(gi):
-            bytes_t[gi] = keep.tile([P, GROUPS[gi], E], U8, name="bytes_%d" % gi)
-            nc.sync.dma_start(out=bytes_t[gi][:], in_=rows_of(hb_rows, gi))
+        def load_bytes(li):
+            bytes_t[li] = keep.tile([P, 4, E], U8, name="bytes_%d" % li)
+            nc.sync.dma_start(out=bytes_t[li][:], in_=rows_of(hb_rows, li))
 
-        def load_x(gi, split=1):
-            n = GROUPS[gi]
-            xt = work.tile([P, n, D], BF16, name="xt", bufs=3)
-            x_t[gi] = xt
+        def load_x(li, split=1):
+            xt = work.tile([P, 4, D], BF16, name="xt", bufs=3)
+            x_t[li] = xt
             for c in range(split):
-                js = slice(c * n // split, (c + 1) * n // split)
-                nc.sync.dma_start(out=xt[:, js, :], in_=rows_of(x_rows, gi)[:, js, :])
+                js = slice(c * 4 // split, (c + 1) * 4 // split)
+                nc.sync.dma_start(out=xt[:, js, :], in_=rows_of(x_rows, li)[:, js, :])
 
         load_bytes(0)
         nc.scalar.dma_start(out=scale_rows[:], in_=h_attn_scale.rearrange("a b k -> (a b k)").partition_broadcast(P))
@@ -126,7 +126,7 @@ def tile_minitransformerlayer_pb_t_kernel(tc, h_attn_bytes, h_attn_scale, x, w_o
         a_scales = {}
 
         def a_product(i):
-            gi, j = group_of[i]
+            gi, j = divmod(i, 4)
             hb = work.tile([P, E], BF16, name="hb", bufs=6)
             hb_t[i] = hb
             nc.vector.tensor_tensor(out=hb[:], in0=bytes_t[gi][:, j, :].bitcast(FP8), in1=scale_rows[:], op=ALU.mult)
@@ -175,7 +175,7 @@ def tile_minitransformerlayer_pb_t_kernel(tc, h_attn_bytes, h_attn_scale, x, w_o
         sums = {}
 
         def residual(i):
-            gi, j = group_of[i]
+            gi, j = divmod(i, 4)
             xm = work.tile([P, D], F32, name="xm", bufs=7)
             sm = work.tile([P, 2], F32, name="sm", bufs=4)
             xm_t[i], sums[i] = xm, sm
@@ -193,24 +193,32 @@ def tile_minitransformerlayer_pb_t_kernel(tc, h_attn_bytes, h_attn_scale, x, w_o
             sm = sums.pop(i)
             nc.vector.tensor_scalar(out=nm[:], in0=sm[:, 0:1], scalar1=sm[:, 1:2], scalar2=-1.0 / D, op0=ALU.add, op1=ALU.mult)
 
+        ss_t = {}
+
         def deviation(i):
             junk = work.tile([P, D], BF16, name="junk", bufs=2)
-            ss = work.tile([P, 1], F32, name="ss", bufs=4)
-            nc.scalar.activation(out=junk[:], in_=xm_t[i][:], func=ACT.Square, bias=nm_t[i][:], scale=1.0, accum_out=ss[:])
-            ve = work.tile([P, 1], F32, name="ve", bufs=4)
-            rs = work.tile([P, 1], F32, name="rs", bufs=6)
-            rs_t[i] = rs
-            nc.gpsimd.tensor_scalar(out=ve[:], in0=ss[:], scalar1=1.0 / D, scalar2=EPS, op0=ALU.mult, op1=ALU.add)
+            if i % RB == 0:
+                ss = work.tile([P, RB], F32, name="ss", bufs=4)
+                ss_t[i // RB] = ss
+            c = i % RB
+            nc.scalar.activation(out=junk[:], in_=xm_t[i][:], func=ACT.Square, bias=nm_t[i][:], scale=1.0, accum_out=ss_t[i // RB][:, c : c + 1])
+
+        def inv_deviation(r):
+            ve = work.tile([P, RB], F32, name="ve", bufs=4)
+            rs = work.tile([P, RB], F32, name="rs", bufs=4)
+            nc.gpsimd.tensor_scalar(out=ve[:], in0=ss_t.pop(r)[:], scalar1=1.0 / D, scalar2=EPS, op0=ALU.mult, op1=ALU.add)
             nc.gpsimd.tensor_tensor(out=rs[:], in0=ve[:], in1=mhalf[:], op=ALU.pow)
+            for c in range(RB):
+                rs_t[RB * r + c] = rs[:, c : c + 1]
 
         def normalize(i):
-            z = work.tile([P, D], F32, name="z", bufs=9)
+            z = work.tile([P, D], F32, name="z", bufs=ZB)
             z_t[i] = z
             eng = nc.vector if Z_ENGINE == "vector" else nc.gpsimd
             eng.tensor_scalar(
                 out=z[:].rearrange("p (t q r) -> p t q r", t=4, r=8),
                 in0=xm_t.pop(i)[:].rearrange("p (q t r) -> p t q r", t=4, r=8),
-                scalar1=nm_t.pop(i)[:], scalar2=rs_t.pop(i)[:], op0=ALU.add, op1=ALU.mult,
+                scalar1=nm_t.pop(i)[:], scalar2=rs_t.pop(i), op0=ALU.add, op1=ALU.mult,
             )
 
         planes = {}
@@ -218,16 +226,24 @@ def tile_minitransformerlayer_pb_t_kernel(tc, h_attn_bytes, h_attn_scale, x, w_o
         h_codes = {}
         h_scales = {}
 
-        def plane(gi, idx, engine):
+        z_bank = {}
+
+        def plane_turn(gi, idx):
+            g, t = divmod(idx, 4)
+            n = GROUPS[gi]
+            bank = psum.tile([P, P * n], F32, name="pz", bufs=2)
+            for j in range(n):
+                c0 = 256 * t + P * g
+                nc.tensor.transpose(bank[:, P * j : P * j + P], z_t[bases[gi] + j][:, c0 : c0 + P], ident[:])
+            z_bank[gi, idx] = bank
+
+        def plane_out(gi, idx, engine):
             g, t = divmod(idx, 4)
             n = GROUPS[gi]
             if t == 0:
                 hp = work.tile([P, 4, P * n], BF16, name="hp", bufs=4)
                 planes[gi, g] = hp
-            bank = psum.tile([P, P * n], F32, name="pz", bufs=2)
-            for j in range(n):
-                c0 = 256 * t + P * g
-                nc.tensor.transpose(bank[:, P * j : P * j + P], z_t[bases[gi] + j][:, c0 : c0 + P], ident[:])
+            bank = z_bank.pop((gi, idx))
             dst = planes[gi, g][:, t, :]
             if engine == "v":
                 nc.vector.tensor_scalar(out=dst, in0=bank[:], scalar1=gb[:, idx : idx + 1], scalar2=gb[:, 8 + idx : 9 + idx], op0=ALU.mult, op1=ALU.add)
@@ -250,6 +266,8 @@ def tile_minitransformerlayer_pb_t_kernel(tc, h_attn_bytes, h_attn_scale, x, w_o
             h_codes[gi, g], h_scales[gi, g] = codes, scales
             quantize(codes[:], scales[:], inter.pop((gi, g))[:])
 
+        u_bank = {}
+
         def mm2(i):
             gi, j = group_of[i]
             bank = psum.tile([P, F], F32, name="pu", bufs=2)
@@ -264,12 +282,12 @@ def tile_minitransformerlayer_pb_t_kernel(tc, h_attn_bytes, h_attn_scale, x, w_o
                     start=(g == 0),
                     stop=(g == 1),
                 )
-            return bank
+            u_bank[i] = bank
 
-        def gelu(i, bank):
-            gi, j = group_of[i]
+        def gelu(i):
+            gi, j = divmod(i, 4)
             act = work.tile([P, F], F32, name="act", bufs=4)
-            nc.scalar.activation(out=act[:], in_=bank[:], func=ACT.Gelu)
+            nc.scalar.activation(out=act[:], in_=u_bank.pop(i)[:], func=ACT.Gelu)
             nc.sync.dma_start(out=rows_of(act_rows, gi)[:, j, :], in_=act[:])
 
         wo_grp = stage.tile([P, D, 4], BF16, name="wo_grp", tag="w8", bufs=3, align_bytes=64)
@@ -311,24 +329,29 @@ def tile_minitransformerlayer_pb_t_kernel(tc, h_attn_bytes, h_attn_scale, x, w_o
                 turn(bank, b, wf_words, 512 * (2 * half + b) + 256 * g)
             empty_words(bank, wf_grp[:, g, 256 * half : 256 * half + 256, :], "s")
 
-        plane_at = {}
+        turn_z_at = {}
+        out_z_at = {}
         inter_at = {}
         quant_at = {}
         mm2_at = {}
+        gelu_at = {}
         last_slot = 0
         for gi, n in enumerate(GROUPS):
-            e = bases[gi] + n - 1 + ZLAG - 1
+            e = bases[gi] + n - 1
             per = 8 // n
-            for s in range(n):
-                plane_at.setdefault(e + 2 + s, []).extend((gi, per * s + k) for k in range(per))
-            half = (n - 1) // 2
-            for g, done in enumerate((e + 2 + half, e + 1 + n)):
-                inter_at.setdefault(done + IL, []).append((gi, g))
-                quant_at.setdefault(done + IL + QL, []).append((gi, g))
+            for k in range(8):
+                at = e + TL + k // per
+                turn_z_at.setdefault(at, []).append((gi, k))
+                out_z_at.setdefault(at + DL, []).append((gi, k))
+            for g in range(2):
+                at = e + TL + (4 * g + 3) // per + DL + IL
+                inter_at.setdefault(at, []).append((gi, g))
+                quant_at.setdefault(at + QL, []).append((gi, g))
             for j in range(n):
-                at = e + 1 + n + IL + QL + ML + j
+                at = e + TL + n - 1 + DL + IL + QL + ML + j
                 mm2_at.setdefault(at, []).append(bases[gi] + j)
-                last_slot = max(last_slot, at)
+                gelu_at.setdefault(at + GL, []).append(bases[gi] + j)
+                last_slot = max(last_slot, at + GL)
 
         product_at = {}
         turn_at = {}
@@ -340,24 +363,36 @@ def tile_minitransformerlayer_pb_t_kernel(tc, h_attn_bytes, h_attn_scale, x, w_o
             product_at.setdefault(ps, []).append(i)
             turn_at.setdefault(ts, []).append(i)
             if i % 2 == 1:
-                empty_at[ts] = i // 2
+                empty_at[ts if i < 6 else ts + 1] = i // 2
                 a_quant_at[min(ts + AQ, i - 2)] = i // 2
 
         for s in range(last_slot + 1):
-            for gi in range(2, len(GROUPS)):
-                if s == max(0, bases[gi] - 7):
-                    load_x(gi)
-                    if gi + 1 < len(GROUPS):
-                        load_bytes(gi + 1)
+            for li in range(2, 8):
+                if s == 4 * li - 7:
+                    load_x(li)
+                    if li < 7:
+                        load_bytes(li + 1)
+            def out_z(some):
+                for gi, idx in some:
+                    plane_out(gi, idx, "v" if idx in (VIDX if gi < VG else VTAIL) else "s")
+
+            done = out_z_at.get(s, [])
+            out_z(done[: len(done) // 2])
+            for i in gelu_at.get(s, []):
+                gelu(i)
+            if s in empty_at and s > 2:
+                a_empty(empty_at[s])
+            out_z(done[len(done) // 2 :])
+            if 0 <= s - 1 < N_TILES:
+                deviation(s - 1)
+                if s % RB == 0:
+                    inv_deviation(s // RB - 1)
+                    for c in range(RB):
+                        normalize(s - RB + c)
             if s in a_quant_at:
                 a_quant(a_quant_at[s])
-            if s + 1 < N_TILES:
-                mm1(s + 1)
-            u_banks = [(i, mm2(i)) for i in mm2_at.get(s, [])]
             if s < N_TILES:
                 residual(s)
-            if 0 <= s - ZLAG < N_TILES:
-                normalize(s - ZLAG)
             for n_p, i in enumerate(product_at.get(s, [])):
                 if n_p == 0:
                     a_product(i)
@@ -368,22 +403,25 @@ def tile_minitransformerlayer_pb_t_kernel(tc, h_attn_bytes, h_attn_scale, x, w_o
             for n_p, i in enumerate(product_at.get(s, [])):
                 if n_p > 0:
                     a_product(i)
-            if WF <= s < WF + 4:
-                wf_turn((s - WF) % 2, (s - WF) // 2)
-            for i in turn_at.get(s, []):
-                a_turn(i)
-            for k, (gi, idx) in enumerate(plane_at.get(s, [])):
-                plane(gi, idx, "v" if (gi >= VG and idx % 8 in VIDX) else "s")
-            for i, bank in u_banks:
-                gelu(i, bank)
-            if s in empty_at:
-                a_empty(empty_at[s])
-            if s < N_TILES:
-                deviation(s)
-            if WF - 2 <= s < WF + 2:
-                wf_permute(s - WF + 2)
             for gi, g in inter_at.get(s, []):
                 interleave(gi, g)
             if s in (WF + 4, WF + 5):
                 g = s - WF - 4
                 quantize(wf_codes[:, g, :], wf_scales[:, g, :], wf_grp[:, g, :, :])
+            if s + 1 < N_TILES:
+                mm1(s + 1)
+            todo = turn_z_at.get(s, [])
+            for gi, idx in todo[: len(todo) // 2]:
+                plane_turn(gi, idx)
+            for i in turn_at.get(s, []):
+                a_turn(i)
+            for i in mm2_at.get(s, []):
+                mm2(i)
+            for gi, idx in todo[len(todo) // 2 :]:
+                plane_turn(gi, idx)
+            if WF - 2 <= s < WF + 2:
+                wf_permute(s - WF + 2)
+            if WF <= s < WF + 4:
+                wf_turn((s - WF) % 2, (s - WF) // 2)
+            if s in empty_at and s <= 2:
+                a_empty(empty_at[s])

@@ -20,12 +20,14 @@ P = 128
 N_TILES = TOKENS // P
 GROUPS = [4,4,4,4,4,4,4,2,2]
 Z_ENGINE = "gpsimd"
-LP, WF = 8, 3
+LP, WF = 6, 2
 AQ = 2
-ZB = 12
-TL, DL, IL, QL, ML, GL = 4, 1, 1, 1, 1, 1
+ZB = 10
+TL, DL, IL, QL, ML, GL = 5, 1, 1, 1, 1, 1
 RB = 2
-VG, VIDX, VTAIL = 6, (), (2, 5, 7)
+ZL = 4
+V_ORDER = (7, 3, 5, 1, 6, 2, 4, 0)
+V_SHARE = (0, 0, 0, 0, 0, 3, 3, 3, 3)
 
 
 def tile_minitransformerlayer_pb_t_kernel(tc, h_attn_bytes, h_attn_scale, x, w_out, w_fc1, g2, b2, out_0, out_1):
@@ -91,13 +93,13 @@ def tile_minitransformerlayer_pb_t_kernel(tc, h_attn_bytes, h_attn_scale, x, w_o
         wo_view = w_out.rearrange("(a p) k -> p a k", p=P)
         for c in range(2):
             nc.sync.dma_start(out=wo_raw[:, 4 * c : 4 * c + 4, :], in_=wo_view[:, 4 * c : 4 * c + 4, :])
+        load_bytes(1)
         load_x(0, 4)
         for v, vec in enumerate((g2, b2)):
             view = vec.rearrange("(g q t r) -> g t q r", g=2, q=16, t=4)
             for g in range(2):
                 r0 = 8 * v + 4 * g
                 nc.scalar.dma_start(out=gb_bf[r0 : r0 + 4, :].rearrange("t (q r) -> t q r", q=16), in_=view[g])
-        load_bytes(1)
         wf_raw = stage.tile([P, 4, D], BF16, name="wf_raw", tag="w8", bufs=3, align_bytes=64)
         nc.sync.dma_start(out=wf_raw[:], in_=w_fc1.rearrange("(a p) k -> p a k", p=P))
         load_x(1)
@@ -133,7 +135,10 @@ def tile_minitransformerlayer_pb_t_kernel(tc, h_attn_bytes, h_attn_scale, x, w_o
 
         def a_turn(i):
             if i % 2 == 0:
-                bank = psum.tile([P, 512], F32, name="pa", bufs=1)
+                if i < 2 or i >= 6:
+                    bank = psum.tile([P, 512], F32, name="pa", bufs=1)
+                else:
+                    bank = psum.tile([P, 512], F32, name="pm", bufs=2)
                 a_bank[i // 2] = bank
             turn(a_bank[i // 2], i % 2, hb_t.pop(i)[:].bitcast(F32), 0)
 
@@ -159,7 +164,7 @@ def tile_minitransformerlayer_pb_t_kernel(tc, h_attn_bytes, h_attn_scale, x, w_o
             cs = slice(P * h, P * h + P)
             m1[i] = []
             for c in range(2):
-                bank = psum.tile([P, 512], F32, name="pm", bufs=3)
+                bank = psum.tile([P, 512], F32, name="pm", bufs=2)
                 m1[i].append(bank)
                 ds = slice(512 * c, 512 * c + 512)
                 nc.tensor.matmul_mx(
@@ -176,7 +181,7 @@ def tile_minitransformerlayer_pb_t_kernel(tc, h_attn_bytes, h_attn_scale, x, w_o
 
         def residual(i):
             gi, j = divmod(i, 4)
-            xm = work.tile([P, D], F32, name="xm", bufs=7)
+            xm = work.tile([P, D], F32, name="xm", bufs=8)
             sm = work.tile([P, 2], F32, name="sm", bufs=4)
             xm_t[i], sums[i] = xm, sm
             for c in range(2):
@@ -188,7 +193,7 @@ def tile_minitransformerlayer_pb_t_kernel(tc, h_attn_bytes, h_attn_scale, x, w_o
             nc.sync.dma_start(out=rows_of(mid_rows, gi)[:, j, :], in_=xm[:])
 
         def neg_mean(i):
-            nm = work.tile([P, 1], F32, name="nm", bufs=6)
+            nm = work.tile([P, 1], F32, name="nm", bufs=7)
             nm_t[i] = nm
             sm = sums.pop(i)
             nc.vector.tensor_scalar(out=nm[:], in0=sm[:, 0:1], scalar1=sm[:, 1:2], scalar2=-1.0 / D, op0=ALU.add, op1=ALU.mult)
@@ -211,6 +216,13 @@ def tile_minitransformerlayer_pb_t_kernel(tc, h_attn_bytes, h_attn_scale, x, w_o
             for c in range(RB):
                 rs_t[RB * r + c] = rs[:, c : c + 1]
 
+        zb_t = {}
+
+        def shift(i):
+            zb = work.tile([P, 1], F32, name="zb", bufs=4)
+            zb_t[i] = zb
+            nc.vector.tensor_tensor(out=zb[:], in0=nm_t.pop(i)[:], in1=rs_t[i], op=ALU.mult)
+
         def normalize(i):
             z = work.tile([P, D], F32, name="z", bufs=ZB)
             z_t[i] = z
@@ -218,7 +230,7 @@ def tile_minitransformerlayer_pb_t_kernel(tc, h_attn_bytes, h_attn_scale, x, w_o
             eng.tensor_scalar(
                 out=z[:].rearrange("p (t q r) -> p t q r", t=4, r=8),
                 in0=xm_t.pop(i)[:].rearrange("p (q t r) -> p t q r", t=4, r=8),
-                scalar1=nm_t.pop(i)[:], scalar2=rs_t.pop(i), op0=ALU.add, op1=ALU.mult,
+                scalar1=rs_t.pop(i), scalar2=zb_t.pop(i)[:], op0=ALU.mult, op1=ALU.add,
             )
 
         planes = {}
@@ -231,7 +243,7 @@ def tile_minitransformerlayer_pb_t_kernel(tc, h_attn_bytes, h_attn_scale, x, w_o
         def plane_turn(gi, idx):
             g, t = divmod(idx, 4)
             n = GROUPS[gi]
-            bank = psum.tile([P, P * n], F32, name="pz", bufs=2)
+            bank = psum.tile([P, P * n], F32, name="pz", bufs=3)
             for j in range(n):
                 c0 = 256 * t + P * g
                 nc.tensor.transpose(bank[:, P * j : P * j + P], z_t[bases[gi] + j][:, c0 : c0 + P], ident[:])
@@ -240,7 +252,7 @@ def tile_minitransformerlayer_pb_t_kernel(tc, h_attn_bytes, h_attn_scale, x, w_o
         def plane_out(gi, idx, engine):
             g, t = divmod(idx, 4)
             n = GROUPS[gi]
-            if t == 0:
+            if (gi, g) not in planes:
                 hp = work.tile([P, 4, P * n], BF16, name="hp", bufs=4)
                 planes[gi, g] = hp
             bank = z_bank.pop((gi, idx))
@@ -286,30 +298,48 @@ def tile_minitransformerlayer_pb_t_kernel(tc, h_attn_bytes, h_attn_scale, x, w_o
 
         def gelu(i):
             gi, j = divmod(i, 4)
-            act = work.tile([P, F], F32, name="act", bufs=4)
+            act = work.tile([P, F], F32, name="act", bufs=6)
             nc.scalar.activation(out=act[:], in_=u_bank.pop(i)[:], func=ACT.Gelu)
             nc.sync.dma_start(out=rows_of(act_rows, gi)[:, j, :], in_=act[:])
 
         wo_grp = stage.tile([P, D, 4], BF16, name="wo_grp", tag="w8", bufs=3, align_bytes=64)
         wo_words = wo_raw[:].rearrange("p a k -> p (a k)").bitcast(F32)
-        for i in range(2):
-            a_product(i)
-        for i in range(2):
-            a_turn(i)
-        for c in range(4):
-            bank = psum.tile([P, 512], F32, name=("pz", "pu")[c % 2], bufs=2)
+        def wo_turn(c):
+            bank = psum.tile([P, 512], F32, name="pz", bufs=3)
             for b in range(2):
                 turn(bank, b, wo_words, 256 * (2 * c + b))
-            empty_words(bank, wo_grp[:, 256 * c : 256 * c + 256, :], "vs"[c % 2])
-            if c == 0:
-                a_empty(0)
-            if c == 1:
-                quantize(wo_codes[:, 0:512], wo_scales[:, 0:512], wo_grp[:, 0:512, :])
-                a_quant(0)
+            return bank
+
+        def wo_empty(bank, c, engine):
+            empty_words(bank, wo_grp[:, 256 * c : 256 * c + 256, :], engine)
+
+        for i in range(4):
+            a_product(i)
+        a_turn(0)
+        a_turn(1)
+        w0 = wo_turn(0)
+        w1 = wo_turn(1)
+        a_empty(0)
+        wo_empty(w0, 0, "v")
+        wo_empty(w1, 1, "s")
+        a_quant(0)
+        w2 = wo_turn(2)
+        w3 = wo_turn(3)
+        a_turn(2)
+        a_turn(3)
+        quantize(wo_codes[:, 0:512], wo_scales[:, 0:512], wo_grp[:, 0:512, :])
+        wo_empty(w2, 2, "v")
+        wo_empty(w3, 3, "s")
+        a_empty(1)
         quantize(wo_codes[:, 512:1024], wo_scales[:, 512:1024], wo_grp[:, 512:1024, :])
+        for i in range(4, 6):
+            a_product(i)
         mm1(0)
+        a_turn(4)
+        a_turn(5)
+        a_empty(2)
         nc.scalar.copy(out=gb_f[:], in_=gb_bf[:])
-        bank = psum.tile([P, 512], F32, name="pz", bufs=2)
+        bank = psum.tile([P, 512], F32, name="pz", bufs=3)
         nc.tensor.transpose(bank[:, 0:P], gb_f[:], ident[:])
         nc.scalar.copy(out=gb[:], in_=bank[:, 0:16])
 
@@ -323,11 +353,17 @@ def tile_minitransformerlayer_pb_t_kernel(tc, h_attn_bytes, h_attn_scale, x, w_o
                 in_=wf_raw[:, a, :].rearrange("p (q t r) -> p q r t", r=8, t=4),
             )
 
+        wf_bank = {}
+        wf_out_at = {}
+
         def wf_turn(g, half):
             bank = psum.tile([P, 512], F32, name="pu", bufs=2)
             for b in range(2):
                 turn(bank, b, wf_words, 512 * (2 * half + b) + 256 * g)
-            empty_words(bank, wf_grp[:, g, 256 * half : 256 * half + 256, :], "s")
+            wf_bank[g, half] = bank
+
+        def wf_empty(g, half):
+            empty_words(wf_bank.pop((g, half)), wf_grp[:, g, 256 * half : 256 * half + 256, :], "s")
 
         turn_z_at = {}
         out_z_at = {}
@@ -357,14 +393,14 @@ def tile_minitransformerlayer_pb_t_kernel(tc, h_attn_bytes, h_attn_scale, x, w_o
         turn_at = {}
         empty_at = {}
         a_quant_at = {}
-        for i in range(2, N_TILES):
-            ps = max(i - LP, i // 2 - 1)
-            ts = 0 if i < 4 else max(i - LP + 1, i // 2)
-            product_at.setdefault(ps, []).append(i)
-            turn_at.setdefault(ts, []).append(i)
+        a_quant_at[0] = 1
+        a_quant_at[2] = 2
+        for i in range(6, N_TILES):
+            product_at.setdefault(i - LP, []).append(i)
+            turn_at.setdefault(i - LP + 1, []).append(i)
             if i % 2 == 1:
-                empty_at[ts if i < 6 else ts + 1] = i // 2
-                a_quant_at[min(ts + AQ, i - 2)] = i // 2
+                empty_at[i - LP + 2] = i // 2
+                a_quant_at[i - LP + 3] = i // 2
 
         for s in range(last_slot + 1):
             for li in range(2, 8):
@@ -374,25 +410,31 @@ def tile_minitransformerlayer_pb_t_kernel(tc, h_attn_bytes, h_attn_scale, x, w_o
                         load_bytes(li + 1)
             def out_z(some):
                 for gi, idx in some:
-                    plane_out(gi, idx, "v" if idx in (VIDX if gi < VG else VTAIL) else "s")
+                    if idx not in V_ORDER[: V_SHARE[gi]]:
+                        plane_out(gi, idx, "s")
+
+            def out_z_v():
+                for gi, idx in out_z_at.get(s, []):
+                    if idx in V_ORDER[: V_SHARE[gi]]:
+                        plane_out(gi, idx, "v")
 
             done = out_z_at.get(s, [])
             out_z(done[: len(done) // 2])
             for i in gelu_at.get(s, []):
                 gelu(i)
-            if s in empty_at and s > 2:
+            if s in empty_at:
                 a_empty(empty_at[s])
+            if s in wf_out_at:
+                wf_empty(*wf_out_at[s])
             out_z(done[len(done) // 2 :])
-            if 0 <= s - 1 < N_TILES:
-                deviation(s - 1)
-                if s % RB == 0:
-                    inv_deviation(s // RB - 1)
-                    for c in range(RB):
-                        normalize(s - RB + c)
-            if s in a_quant_at:
-                a_quant(a_quant_at[s])
+            if 0 <= s - ZL < N_TILES:
+                shift(s - ZL)
+                normalize(s - ZL)
             if s < N_TILES:
                 residual(s)
+            out_z_v()
+            if s in a_quant_at:
+                a_quant(a_quant_at[s])
             for n_p, i in enumerate(product_at.get(s, [])):
                 if n_p == 0:
                     a_product(i)
@@ -405,11 +447,13 @@ def tile_minitransformerlayer_pb_t_kernel(tc, h_attn_bytes, h_attn_scale, x, w_o
                     a_product(i)
             for gi, g in inter_at.get(s, []):
                 interleave(gi, g)
-            if s in (WF + 4, WF + 5):
-                g = s - WF - 4
+            if s in (WF + 5, WF + 6):
+                g = s - WF - 5
                 quantize(wf_codes[:, g, :], wf_scales[:, g, :], wf_grp[:, g, :, :])
-            if s + 1 < N_TILES:
-                mm1(s + 1)
+            if 0 <= s - 1 < N_TILES:
+                deviation(s - 1)
+                if s % RB == 0:
+                    inv_deviation(s // RB - 1)
             todo = turn_z_at.get(s, [])
             for gi, idx in todo[: len(todo) // 2]:
                 plane_turn(gi, idx)
@@ -419,9 +463,10 @@ def tile_minitransformerlayer_pb_t_kernel(tc, h_attn_bytes, h_attn_scale, x, w_o
                 mm2(i)
             for gi, idx in todo[len(todo) // 2 :]:
                 plane_turn(gi, idx)
-            if WF - 2 <= s < WF + 2:
-                wf_permute(s - WF + 2)
+            if s + 1 < N_TILES:
+                mm1(s + 1)
+            if s < 4:
+                wf_permute(s)
             if WF <= s < WF + 4:
                 wf_turn((s - WF) % 2, (s - WF) // 2)
-            if s in empty_at and s <= 2:
-                a_empty(empty_at[s])
+                wf_out_at[s + 1] = ((s - WF) % 2, (s - WF) // 2)

@@ -27,7 +27,8 @@ TL, DL, IL, QL, ML, GL = 5, 1, 1, 1, 1, 1
 RB = 2
 ZL = 4
 V_ORDER = (7, 3, 5, 1, 6, 2, 4, 0)
-V_SHARE = (0, 0, 0, 0, 0, 3, 3, 3, 3)
+S_INTER = ()
+V_SHARE = (0, 0, 0, 0, 1, 3, 4, 4, 4)
 
 
 def tile_minitransformerlayer_pb_t_kernel(tc, h_attn_bytes, h_attn_scale, x, w_out, w_fc1, g2, b2, out_0, out_1):
@@ -216,13 +217,6 @@ def tile_minitransformerlayer_pb_t_kernel(tc, h_attn_bytes, h_attn_scale, x, w_o
             for c in range(RB):
                 rs_t[RB * r + c] = rs[:, c : c + 1]
 
-        zb_t = {}
-
-        def shift(i):
-            zb = work.tile([P, 1], F32, name="zb", bufs=4)
-            zb_t[i] = zb
-            nc.vector.tensor_tensor(out=zb[:], in0=nm_t.pop(i)[:], in1=rs_t[i], op=ALU.mult)
-
         def normalize(i):
             z = work.tile([P, D], F32, name="z", bufs=ZB)
             z_t[i] = z
@@ -230,7 +224,7 @@ def tile_minitransformerlayer_pb_t_kernel(tc, h_attn_bytes, h_attn_scale, x, w_o
             eng.tensor_scalar(
                 out=z[:].rearrange("p (t q r) -> p t q r", t=4, r=8),
                 in0=xm_t.pop(i)[:].rearrange("p (q t r) -> p t q r", t=4, r=8),
-                scalar1=rs_t.pop(i), scalar2=zb_t.pop(i)[:], op0=ALU.mult, op1=ALU.add,
+                scalar1=nm_t.pop(i)[:], scalar2=rs_t.pop(i), op0=ALU.add, op1=ALU.mult,
             )
 
         planes = {}
@@ -244,6 +238,8 @@ def tile_minitransformerlayer_pb_t_kernel(tc, h_attn_bytes, h_attn_scale, x, w_o
             g, t = divmod(idx, 4)
             n = GROUPS[gi]
             bank = psum.tile([P, P * n], F32, name="pz", bufs=3)
+            if idx % 2 == 1:
+                nc.tensor.matmul(bank[:, 0:P], lhsT=ident[:], rhs=ident[:], start=True, stop=True)
             for j in range(n):
                 c0 = 256 * t + P * g
                 nc.tensor.transpose(bank[:, P * j : P * j + P], z_t[bases[gi] + j][:, c0 : c0 + P], ident[:])
@@ -266,7 +262,8 @@ def tile_minitransformerlayer_pb_t_kernel(tc, h_attn_bytes, h_attn_scale, x, w_o
             n = GROUPS[gi]
             hi = work.tile([P, P * n, 4], BF16, name="hi", bufs=3, align_bytes=64)
             inter[gi, g] = hi
-            nc.vector.tensor_copy(
+            copy = nc.scalar.copy if 2 * gi + g in S_INTER else nc.vector.tensor_copy
+            copy(
                 out=hi[:].rearrange("p (c i) t -> p c t i", i=4),
                 in_=planes.pop((gi, g))[:].rearrange("p t (c i) -> p c t i", i=4),
             )
@@ -313,6 +310,9 @@ def tile_minitransformerlayer_pb_t_kernel(tc, h_attn_bytes, h_attn_scale, x, w_o
         def wo_empty(bank, c, engine):
             empty_words(bank, wo_grp[:, 256 * c : 256 * c + 256, :], engine)
 
+        warm_bank = psum.tile([P, 512], F32, name="pz", bufs=3)
+        for i in range(6):
+            nc.tensor.matmul(warm_bank[:, 0:P], lhsT=ident[:], rhs=ident[:], start=True, stop=True)
         for i in range(4):
             a_product(i)
         a_turn(0)
@@ -418,17 +418,16 @@ def tile_minitransformerlayer_pb_t_kernel(tc, h_attn_bytes, h_attn_scale, x, w_o
                     if idx in V_ORDER[: V_SHARE[gi]]:
                         plane_out(gi, idx, "v")
 
+            if s in empty_at:
+                a_empty(empty_at[s])
             done = out_z_at.get(s, [])
             out_z(done[: len(done) // 2])
             for i in gelu_at.get(s, []):
                 gelu(i)
-            if s in empty_at:
-                a_empty(empty_at[s])
             if s in wf_out_at:
                 wf_empty(*wf_out_at[s])
             out_z(done[len(done) // 2 :])
             if 0 <= s - ZL < N_TILES:
-                shift(s - ZL)
                 normalize(s - ZL)
             if s < N_TILES:
                 residual(s)
@@ -455,16 +454,16 @@ def tile_minitransformerlayer_pb_t_kernel(tc, h_attn_bytes, h_attn_scale, x, w_o
                 if s % RB == 0:
                     inv_deviation(s // RB - 1)
             todo = turn_z_at.get(s, [])
-            for gi, idx in todo[: len(todo) // 2]:
-                plane_turn(gi, idx)
-            for i in turn_at.get(s, []):
-                a_turn(i)
             for i in mm2_at.get(s, []):
                 mm2(i)
-            for gi, idx in todo[len(todo) // 2 :]:
+            for gi, idx in todo[: len(todo) // 2]:
                 plane_turn(gi, idx)
             if s + 1 < N_TILES:
                 mm1(s + 1)
+            for i in turn_at.get(s, []):
+                a_turn(i)
+            for gi, idx in todo[len(todo) // 2 :]:
+                plane_turn(gi, idx)
             if s < 4:
                 wf_permute(s)
             if WF <= s < WF + 4:

from contextlib import ExitStack

import concourse.mybir as mybir
from concourse.masks import make_identity

TOKENS, D, E, F = 4096, 1024, 512, 512
EPS = 1e-5
FLOPS = 2 * TOKENS * E * D + 2 * TOKENS * D * F

F32 = mybir.dt.float32
BF16 = mybir.dt.bfloat16
U32 = mybir.dt.uint32
U8 = mybir.dt.uint8
FP8 = mybir.dt.float8_e4m3fn
FP8X4 = mybir.dt.float8_e4m3fn_x4
ALU = mybir.AluOpType
ACT = mybir.ActivationFunctionType

P = 128
N_TILES = TOKENS // P
GROUPS = [4,4,4,4,4,4,4,2,2]
Z_ENGINE = "gpsimd"
LP, WF = 6, 2
AQ = 2
ZB = 10
TL, DL, IL, QL, ML, GL = 5, 1, 1, 1, 1, 1
RB = 2
ZL = 4
V_ORDER = (7, 3, 5, 1, 6, 2, 4, 0)
S_INTER = ()
V_SHARE = (0, 0, 0, 0, 1, 3, 4, 4, 4)


def tile_minitransformerlayer_pb_t_kernel(tc, h_attn_bytes, h_attn_scale, x, w_out, w_fc1, g2, b2, out_0, out_1):
    nc = tc.nc
    hb_rows = h_attn_bytes.flatten_outer_dims()
    x_rows = x.flatten_outer_dims()
    mid_rows = out_0.flatten_outer_dims()
    act_rows = out_1.flatten_outer_dims()

    bases = []
    base = 0
    for n in GROUPS:
        bases.append(base)
        base += n

    group_of = {}
    for gi, n in enumerate(GROUPS):
        for j in range(n):
            group_of[bases[gi] + j] = (gi, j)

    with ExitStack() as ctx:
        keep = ctx.enter_context(tc.tile_pool(name="keep", bufs=1))
        stage = ctx.enter_context(tc.tile_pool(name="stage", bufs=1))
        work = ctx.enter_context(tc.tile_pool(name="work", bufs=2))
        psum = ctx.enter_context(tc.psum_pool(name="psum", bufs=2))
        ctx.enter_context(tc.manual_schedule())

        ident = keep.tile([P, P], F32, name="ident")
        make_identity(nc, ident[:])
        scale_rows = keep.tile([P, E], F32, name="scale_rows")
        gb_bf = keep.tile([P, P], BF16, name="gb_bf")
        gb_f = keep.tile([P, P], F32, name="gb_f")
        gb = keep.tile([P, 16], F32, name="gb")
        mhalf = keep.tile([P, RB], F32, name="mhalf")
        nc.gpsimd.memset(gb_bf[:], 0.0)
        nc.gpsimd.memset(mhalf[:], -0.5)

        wo_codes = keep.tile([P, D], U32, name="wo_codes", align_bytes=64)
        wo_scales = keep.tile([P, D], U8, name="wo_scales", align_bytes=64)
        wf_codes = keep.tile([P, 2, F], U32, name="wf_codes", align_bytes=64)
        wf_scales = keep.tile([P, 2, F], U8, name="wf_scales", align_bytes=64)

        bytes_t = {}
        x_t = {}

        def rows_of(dram, li):
            return dram[4 * P * li : 4 * P * (li + 1), :].rearrange("(p j) k -> p j k", j=4)

        def load_bytes(li):
            bytes_t[li] = keep.tile([P, 4, E], U8, name="bytes_%d" % li)
            nc.sync.dma_start(out=bytes_t[li][:], in_=rows_of(hb_rows, li))

        def load_x(li, split=1):
            xt = work.tile([P, 4, D], BF16, name="xt", bufs=3)
            x_t[li] = xt
            for c in range(split):
                js = slice(c * 4 // split, (c + 1) * 4 // split)
                nc.sync.dma_start(out=xt[:, js, :], in_=rows_of(x_rows, li)[:, js, :])

        load_bytes(0)
        nc.scalar.dma_start(out=scale_rows[:], in_=h_attn_scale.rearrange("a b k -> (a b k)").partition_broadcast(P))
        wo_raw = stage.tile([P, 8, E], BF16, name="wo_raw", tag="w8", bufs=3, align_bytes=64)
        wo_view = w_out.rearrange("(a p) k -> p a k", p=P)
        for c in range(2):
            nc.sync.dma_start(out=wo_raw[:, 4 * c : 4 * c + 4, :], in_=wo_view[:, 4 * c : 4 * c + 4, :])
        load_bytes(1)
        load_x(0, 4)
        for v, vec in enumerate((g2, b2)):
            view = vec.rearrange("(g q t r) -> g t q r", g=2, q=16, t=4)
            for g in range(2):
                r0 = 8 * v + 4 * g
                nc.scalar.dma_start(out=gb_bf[r0 : r0 + 4, :].rearrange("t (q r) -> t q r", q=16), in_=view[g])
        wf_raw = stage.tile([P, 4, D], BF16, name="wf_raw", tag="w8", bufs=3, align_bytes=64)
        nc.sync.dma_start(out=wf_raw[:], in_=w_fc1.rearrange("(a p) k -> p a k", p=P))
        load_x(1)
        load_bytes(2)

        def turn(bank, slot, words, start):
            for u in range(2):
                c0 = P * (2 * slot + u)
                nc.tensor.transpose(bank[:, c0 : c0 + P], words[:, start + u : start + 256 : 2], ident[:])

        def empty_words(bank, dst, engine):
            out = dst.rearrange("p n j -> p (n j)").bitcast(F32).rearrange("p (b r u) -> p b r u", b=2, u=2)
            in_ = bank[:].rearrange("p (b u r) -> p b r u", b=2, u=2)
            if engine == "v":
                nc.vector.tensor_copy(out=out, in_=in_)
            else:
                nc.scalar.copy(out=out, in_=in_)

        def quantize(codes, scales, src):
            nc.vector.quantize_mx(out=codes.bitcast(FP8X4), scales=scales, in_=src.rearrange("p n j -> p (n j)"))

        hb_t = {}
        a_bank = {}
        a_grp = {}
        a_codes = {}
        a_scales = {}

        def a_product(i):
            gi, j = divmod(i, 4)
            hb = work.tile([P, E], BF16, name="hb", bufs=6)
            hb_t[i] = hb
            nc.vector.tensor_tensor(out=hb[:], in0=bytes_t[gi][:, j, :].bitcast(FP8), in1=scale_rows[:], op=ALU.mult)

        def a_turn(i):
            if i % 2 == 0:
                if i < 2 or i >= 6:
                    bank = psum.tile([P, 512], F32, name="pa", bufs=1)
                else:
                    bank = psum.tile([P, 512], F32, name="pm", bufs=2)
                a_bank[i // 2] = bank
            turn(a_bank[i // 2], i % 2, hb_t.pop(i)[:].bitcast(F32), 0)

        def a_empty(pair, engine="s"):
            grp = work.tile([P, 256, 4], BF16, name="a_grp", bufs=3, align_bytes=64)
            a_grp[pair] = grp
            empty_words(a_bank.pop(pair), grp[:], engine)

        def a_quant(pair):
            codes = work.tile([P, 256], U32, name="a_codes", bufs=3, align_bytes=64)
            scales = work.tile([P, 256], U8, name="a_scales", bufs=3, align_bytes=64)
            a_codes[pair], a_scales[pair] = codes, scales
            quantize(codes[:], scales[:], a_grp.pop(pair)[:])

        m1 = {}
        xm_t = {}
        nm_t = {}
        rs_t = {}
        z_t = {}

        def mm1(i):
            pair, h = divmod(i, 2)
            cs = slice(P * h, P * h + P)
            m1[i] = []
            for c in range(2):
                bank = psum.tile([P, 512], F32, name="pm", bufs=2)
                m1[i].append(bank)
                ds = slice(512 * c, 512 * c + 512)
                nc.tensor.matmul_mx(
                    out=bank[:],
                    lhsT=a_codes[pair][:, cs].bitcast(FP8X4),
                    lhsT_scale=a_scales[pair][:, cs],
                    rhs=wo_codes[:, ds].bitcast(FP8X4),
                    rhs_scale=wo_scales[:, ds],
                    start=True,
                    stop=True,
                )

        sums = {}

        def residual(i):
            gi, j = divmod(i, 4)
            xm = work.tile([P, D], F32, name="xm", bufs=8)
            sm = work.tile([P, 2], F32, name="sm", bufs=4)
            xm_t[i], sums[i] = xm, sm
            for c in range(2):
                ds = slice(512 * c, 512 * c + 512)
                nc.vector.scalar_tensor_tensor(
                    out=xm[:, ds], in0=m1[i][c][:], scalar=1.0, in1=x_t[gi][:, j, ds],
                    op0=ALU.mult, op1=ALU.add, accum_out=sm[:, c : c + 1],
                )
            nc.sync.dma_start(out=rows_of(mid_rows, gi)[:, j, :], in_=xm[:])

        def neg_mean(i):
            nm = work.tile([P, 1], F32, name="nm", bufs=7)
            nm_t[i] = nm
            sm = sums.pop(i)
            nc.vector.tensor_scalar(out=nm[:], in0=sm[:, 0:1], scalar1=sm[:, 1:2], scalar2=-1.0 / D, op0=ALU.add, op1=ALU.mult)

        ss_t = {}

        def deviation(i):
            junk = work.tile([P, D], BF16, name="junk", bufs=2)
            if i % RB == 0:
                ss = work.tile([P, RB], F32, name="ss", bufs=4)
                ss_t[i // RB] = ss
            c = i % RB
            nc.scalar.activation(out=junk[:], in_=xm_t[i][:], func=ACT.Square, bias=nm_t[i][:], scale=1.0, accum_out=ss_t[i // RB][:, c : c + 1])

        def inv_deviation(r):
            ve = work.tile([P, RB], F32, name="ve", bufs=4)
            rs = work.tile([P, RB], F32, name="rs", bufs=4)
            nc.gpsimd.tensor_scalar(out=ve[:], in0=ss_t.pop(r)[:], scalar1=1.0 / D, scalar2=EPS, op0=ALU.mult, op1=ALU.add)
            nc.gpsimd.tensor_tensor(out=rs[:], in0=ve[:], in1=mhalf[:], op=ALU.pow)
            for c in range(RB):
                rs_t[RB * r + c] = rs[:, c : c + 1]

        def normalize(i):
            z = work.tile([P, D], F32, name="z", bufs=ZB)
            z_t[i] = z
            eng = nc.vector if Z_ENGINE == "vector" else nc.gpsimd
            eng.tensor_scalar(
                out=z[:].rearrange("p (t q r) -> p t q r", t=4, r=8),
                in0=xm_t.pop(i)[:].rearrange("p (q t r) -> p t q r", t=4, r=8),
                scalar1=nm_t.pop(i)[:], scalar2=rs_t.pop(i), op0=ALU.add, op1=ALU.mult,
            )

        planes = {}
        inter = {}
        h_codes = {}
        h_scales = {}

        z_bank = {}

        def plane_turn(gi, idx):
            g, t = divmod(idx, 4)
            n = GROUPS[gi]
            bank = psum.tile([P, P * n], F32, name="pz", bufs=3)
            if idx % 2 == 1:
                nc.tensor.matmul(bank[:, 0:P], lhsT=ident[:], rhs=ident[:], start=True, stop=True)
            for j in range(n):
                c0 = 256 * t + P * g
                nc.tensor.transpose(bank[:, P * j : P * j + P], z_t[bases[gi] + j][:, c0 : c0 + P], ident[:])
            z_bank[gi, idx] = bank

        def plane_out(gi, idx, engine):
            g, t = divmod(idx, 4)
            n = GROUPS[gi]
            if (gi, g) not in planes:
                hp = work.tile([P, 4, P * n], BF16, name="hp", bufs=4)
                planes[gi, g] = hp
            bank = z_bank.pop((gi, idx))
            dst = planes[gi, g][:, t, :]
            if engine == "v":
                nc.vector.tensor_scalar(out=dst, in0=bank[:], scalar1=gb[:, idx : idx + 1], scalar2=gb[:, 8 + idx : 9 + idx], op0=ALU.mult, op1=ALU.add)
            else:
                nc.scalar.activation(out=dst, in_=bank[:], func=ACT.Identity, bias=gb[:, 8 + idx : 9 + idx], scale=gb[:, idx : idx + 1])

        def interleave(gi, g):
            n = GROUPS[gi]
            hi = work.tile([P, P * n, 4], BF16, name="hi", bufs=3, align_bytes=64)
            inter[gi, g] = hi
            copy = nc.scalar.copy if 2 * gi + g in S_INTER else nc.vector.tensor_copy
            copy(
                out=hi[:].rearrange("p (c i) t -> p c t i", i=4),
                in_=planes.pop((gi, g))[:].rearrange("p t (c i) -> p c t i", i=4),
            )

        def h_quant(gi, g):
            n = GROUPS[gi]
            codes = work.tile([P, P * n], U32, name="h_codes", bufs=6, align_bytes=64)
            scales = work.tile([P, P * n], U8, name="h_scales", bufs=6, align_bytes=64)
            h_codes[gi, g], h_scales[gi, g] = codes, scales
            quantize(codes[:], scales[:], inter.pop((gi, g))[:])

        u_bank = {}

        def mm2(i):
            gi, j = group_of[i]
            bank = psum.tile([P, F], F32, name="pu", bufs=2)
            cs = slice(P * j, P * j + P)
            for g in range(2):
                nc.tensor.matmul_mx(
                    out=bank[:],
                    lhsT=h_codes[gi, g][:, cs].bitcast(FP8X4),
                    lhsT_scale=h_scales[gi, g][:, cs],
                    rhs=wf_codes[:, g, :].bitcast(FP8X4),
                    rhs_scale=wf_scales[:, g, :],
                    start=(g == 0),
                    stop=(g == 1),
                )
            u_bank[i] = bank

        def gelu(i):
            gi, j = divmod(i, 4)
            act = work.tile([P, F], F32, name="act", bufs=6)
            nc.scalar.activation(out=act[:], in_=u_bank.pop(i)[:], func=ACT.Gelu)
            nc.sync.dma_start(out=rows_of(act_rows, gi)[:, j, :], in_=act[:])

        wo_grp = stage.tile([P, D, 4], BF16, name="wo_grp", tag="w8", bufs=3, align_bytes=64)
        wo_words = wo_raw[:].rearrange("p a k -> p (a k)").bitcast(F32)
        def wo_turn(c):
            bank = psum.tile([P, 512], F32, name="pz", bufs=3)
            for b in range(2):
                turn(bank, b, wo_words, 256 * (2 * c + b))
            return bank

        def wo_empty(bank, c, engine):
            empty_words(bank, wo_grp[:, 256 * c : 256 * c + 256, :], engine)

        warm_bank = psum.tile([P, 512], F32, name="pz", bufs=3)
        for i in range(6):
            nc.tensor.matmul(warm_bank[:, 0:P], lhsT=ident[:], rhs=ident[:], start=True, stop=True)
        for i in range(4):
            a_product(i)
        a_turn(0)
        a_turn(1)
        w0 = wo_turn(0)
        w1 = wo_turn(1)
        a_empty(0)
        wo_empty(w0, 0, "v")
        wo_empty(w1, 1, "s")
        a_quant(0)
        w2 = wo_turn(2)
        w3 = wo_turn(3)
        a_turn(2)
        a_turn(3)
        quantize(wo_codes[:, 0:512], wo_scales[:, 0:512], wo_grp[:, 0:512, :])
        wo_empty(w2, 2, "v")
        wo_empty(w3, 3, "s")
        a_empty(1)
        quantize(wo_codes[:, 512:1024], wo_scales[:, 512:1024], wo_grp[:, 512:1024, :])
        for i in range(4, 6):
            a_product(i)
        mm1(0)
        a_turn(4)
        a_turn(5)
        a_empty(2)
        nc.scalar.copy(out=gb_f[:], in_=gb_bf[:])
        bank = psum.tile([P, 512], F32, name="pz", bufs=3)
        nc.tensor.transpose(bank[:, 0:P], gb_f[:], ident[:])
        nc.scalar.copy(out=gb[:], in_=bank[:, 0:16])

        wf_perm = stage.tile([P, 4, D], BF16, name="wf_perm", tag="w8", bufs=3, align_bytes=64)
        wf_grp = stage.tile([P, 2, F, 4], BF16, name="wf_grp", tag="w8", bufs=3, align_bytes=64)
        wf_words = wf_perm[:].rearrange("p a k -> p (a k)").bitcast(F32)

        def wf_permute(a):
            nc.scalar.copy(
                out=wf_perm[:, a, :].rearrange("p (q r t) -> p q r t", r=8, t=4),
                in_=wf_raw[:, a, :].rearrange("p (q t r) -> p q r t", r=8, t=4),
            )

        wf_bank = {}
        wf_out_at = {}

        def wf_turn(g, half):
            bank = psum.tile([P, 512], F32, name="pu", bufs=2)
            for b in range(2):
                turn(bank, b, wf_words, 512 * (2 * half + b) + 256 * g)
            wf_bank[g, half] = bank

        def wf_empty(g, half):
            empty_words(wf_bank.pop((g, half)), wf_grp[:, g, 256 * half : 256 * half + 256, :], "s")

        turn_z_at = {}
        out_z_at = {}
        inter_at = {}
        quant_at = {}
        mm2_at = {}
        gelu_at = {}
        last_slot = 0
        for gi, n in enumerate(GROUPS):
            e = bases[gi] + n - 1
            per = 8 // n
            for k in range(8):
                at = e + TL + k // per
                turn_z_at.setdefault(at, []).append((gi, k))
                out_z_at.setdefault(at + DL, []).append((gi, k))
            for g in range(2):
                at = e + TL + (4 * g + 3) // per + DL + IL
                inter_at.setdefault(at, []).append((gi, g))
                quant_at.setdefault(at + QL, []).append((gi, g))
            for j in range(n):
                at = e + TL + n - 1 + DL + IL + QL + ML + j
                mm2_at.setdefault(at, []).append(bases[gi] + j)
                gelu_at.setdefault(at + GL, []).append(bases[gi] + j)
                last_slot = max(last_slot, at + GL)

        product_at = {}
        turn_at = {}
        empty_at = {}
        a_quant_at = {}
        a_quant_at[0] = 1
        a_quant_at[2] = 2
        for i in range(6, N_TILES):
            product_at.setdefault(i - LP, []).append(i)
            turn_at.setdefault(i - LP + 1, []).append(i)
            if i % 2 == 1:
                empty_at[i - LP + 2] = i // 2
                a_quant_at[i - LP + 3] = i // 2

        for s in range(last_slot + 1):
            for li in range(2, 8):
                if s == 4 * li - 7:
                    load_x(li)
                    if li < 7:
                        load_bytes(li + 1)
            def out_z(some):
                for gi, idx in some:
                    if idx not in V_ORDER[: V_SHARE[gi]]:
                        plane_out(gi, idx, "s")

            def out_z_v():
                for gi, idx in out_z_at.get(s, []):
                    if idx in V_ORDER[: V_SHARE[gi]]:
                        plane_out(gi, idx, "v")

            if s in empty_at:
                a_empty(empty_at[s])
            done = out_z_at.get(s, [])
            out_z(done[: len(done) // 2])
            for i in gelu_at.get(s, []):
                gelu(i)
            if s in wf_out_at:
                wf_empty(*wf_out_at[s])
            out_z(done[len(done) // 2 :])
            if 0 <= s - ZL < N_TILES:
                normalize(s - ZL)
            if s < N_TILES:
                residual(s)
            out_z_v()
            if s in a_quant_at:
                a_quant(a_quant_at[s])
            for n_p, i in enumerate(product_at.get(s, [])):
                if n_p == 0:
                    a_product(i)
            if s < N_TILES:
                neg_mean(s)
            for gi, g in quant_at.get(s, []):
                h_quant(gi, g)
            for n_p, i in enumerate(product_at.get(s, [])):
                if n_p > 0:
                    a_product(i)
            for gi, g in inter_at.get(s, []):
                interleave(gi, g)
            if s in (WF + 5, WF + 6):
                g = s - WF - 5
                quantize(wf_codes[:, g, :], wf_scales[:, g, :], wf_grp[:, g, :, :])
            if 0 <= s - 1 < N_TILES:
                deviation(s - 1)
                if s % RB == 0:
                    inv_deviation(s // RB - 1)
            todo = turn_z_at.get(s, [])
            for i in mm2_at.get(s, []):
                mm2(i)
            for gi, idx in todo[: len(todo) // 2]:
                plane_turn(gi, idx)
            if s + 1 < N_TILES:
                mm1(s + 1)
            for i in turn_at.get(s, []):
                a_turn(i)
            for gi, idx in todo[len(todo) // 2 :]:
                plane_turn(gi, idx)
            if s < 4:
                wf_permute(s)
            if WF <= s < WF + 4:
                wf_turn((s - WF) % 2, (s - WF) // 2)
                wf_out_at[s + 1] = ((s - WF) % 2, (s - WF) // 2)
